import numpy as np
import ml_dtypes

BF16 = ml_dtypes.bfloat16


def bf(x):
    return np.asarray(x, np.float32).astype(BF16)


def f32(x):
    return np.asarray(x, np.float32)


def f64(x):
    return np.asarray(x).astype(np.float64)


def striped(idx):
    return np.tile(idx.reshape(-1, 16).T, (8, 1))


C, S, N, K, R, L, B = 256, 2048, 8192, 4, 2048, 16, 128
PE_BASE = 10000.0


def pos_table():
    pos = np.arange(L, dtype=np.float64)[None, :]
    div = np.exp(np.arange(0, C, 2, dtype=np.float64) * (-np.log(PE_BASE) / C))[:, None]
    pe = np.zeros((C, L), np.float64)
    pe[0::2, :] = np.sin(div * pos)
    pe[1::2, :] = np.cos(div * pos)
    return pe


def setup_inputs():
    return {"tab": f32(np.random.standard_normal((C, S))), "w": f32(np.random.uniform(0.0, 1.0, (1, N))), "pe": f32(pos_table()), "offs": striped(np.concatenate([np.random.permutation(S) for _ in range(K)]))}


def reference(tab, w, pe, offs):
    idx = offs[:16].T.reshape(-1)
    prod = f64(tab)[:, idx] * f64(w)
    return prod.reshape(C, K, R).sum(axis=1) + np.repeat(f64(pe), B, axis=1)

@@ -1,0 +1,73 @@
+import concourse.masks as masks
+import concourse.mybir as mybir
+
+F32 = mybir.dt.float32
+U16 = mybir.dt.uint16
+
+P = 128
+C, S = 256, 2048
+K, R = 4, 2048
+N = K * R
+L, B = 16, 128
+BLOCKS = C // P
+PIECE = 512
+PIECES = R // PIECE
+STEPS = PIECE // B
+
+FLOPS = 2 * C * N
+
+
+def tile_progwalktokembedwithval_kernel(tc, tab, w, pe, offs, out):
+    nc = tc.nc
+    w_row = w.rearrange("o n -> (o n)")
+
+    with (
+        tc.tile_pool(name="held", bufs=1) as held,
+        tc.tile_pool(name="products", bufs=4) as products,
+        tc.tile_pool(name="results", bufs=2) as results,
+        tc.psum_pool(name="sums", bufs=2) as sums,
+    ):
+        offsets = held.tile([P, N // 16], U16, name="offsets")
+        nc.sync.dma_start(offsets[:], offs)
+
+        tables = [held.tile([P, S], F32, name=f"table{b}") for b in range(BLOCKS)]
+        encodings = [held.tile([P, L], F32, name=f"encoding{b}") for b in range(BLOCKS)]
+        weights = [[held.tile([P, PIECE], F32, name=f"weights{k}_{i}") for i in range(PIECES)] for k in range(K)]
+
+        nc.sync.dma_start(tables[0][:], tab[0:P, :])
+        for i in range(PIECES):
+            for k in range(K):
+                first = k * R + i * PIECE
+                nc.sync.dma_start(weights[k][i][:], w_row[first : first + PIECE].partition_broadcast(P))
+            if i == 0:
+                for b in range(BLOCKS):
+                    nc.sync.dma_start(encodings[b][:], pe[b * P : (b + 1) * P, :])
+        nc.sync.dma_start(tables[1][:], tab[P : 2 * P, :])
+
+        identity = held.tile([P, P], F32, name="identity")
+        masks.make_identity(nc, identity[:])
+
+        for b in range(BLOCKS):
+            for i in range(PIECES):
+                total = sums.tile([P, PIECE], F32, name="total")
+                for k in range(K):
+                    first = (k * R + i * PIECE) // 16
+                    product = products.tile([P, PIECE], F32, name="product")
+                    nc.vector.tensor_tensor(
+                        product[:],
+                        tables[b][:].indirect(offsets[:, first : first + PIECE // 16]),
+                        weights[k][i][:],
+                        mybir.AluOpType.mult,
+                    )
+                    nc.tensor.matmul(total[:], identity[:], product[:], start=(k == 0), stop=(k == K - 1))
+
+                result = results.tile([P, PIECE], F32, name="result")
+                for s in range(STEPS):
+                    step = i * STEPS + s
+                    nc.scalar.activation(
+                        result[:, s * B : (s + 1) * B],
+                        total[:, s * B : (s + 1) * B],
+                        mybir.ActivationFunctionType.Identity,
+                        bias=encodings[b][:, step : step + 1],
+                    )
+                nc.sync.dma_start(out[b * P : (b + 1) * P, i * PIECE : (i + 1) * PIECE], result[:])

@@ -40,15 +40,15 @@ def tile_progwalktokembedwithval_kernel(tc, tab, w, pe, offs, out):
                 first = k * R + i * PIECE
                 nc.sync.dma_start(weights[k][i][:], w_row[first : first + PIECE].partition_broadcast(P))
             if i == 0:
+                nc.sync.dma_start(tables[1][:], tab[P : 2 * P, :])
                 for b in range(BLOCKS):
                     nc.sync.dma_start(encodings[b][:], pe[b * P : (b + 1) * P, :])
-        nc.sync.dma_start(tables[1][:], tab[P : 2 * P, :])
 
         identity = held.tile([P, P], F32, name="identity")
         masks.make_identity(nc, identity[:])
 
-        for b in range(BLOCKS):
-            for i in range(PIECES):
+        for i in range(PIECES):
+            for b in range(BLOCKS):
                 total = sums.tile([P, PIECE], F32, name="total")
                 for k in range(K):
                     first = (k * R + i * PIECE) // 16

@@ -50,6 +50,7 @@ def tile_progwalktokembedwithval_kernel(tc, tab, w, pe, offs, out):
         for i in range(PIECES):
             for b in range(BLOCKS):
                 total = sums.tile([P, PIECE], F32, name="total")
+                addends = []
                 for k in range(K):
                     first = (k * R + i * PIECE) // 16
                     product = products.tile([P, PIECE], F32, name="product")
@@ -59,7 +60,13 @@ def tile_progwalktokembedwithval_kernel(tc, tab, w, pe, offs, out):
                         weights[k][i][:],
                         mybir.AluOpType.mult,
                     )
-                    nc.tensor.matmul(total[:], identity[:], product[:], start=(k == 0), stop=(k == K - 1))
+                    addends.append(product)
+                    if k == 1:
+                        pair = products.tile([P, PIECE], F32, name="pair")
+                        nc.vector.tensor_tensor(pair[:], addends[0][:], addends[1][:], mybir.AluOpType.add)
+                        addends = [pair]
+                    if k >= 1:
+                        nc.tensor.matmul(total[:], identity[:], addends[-1][:], start=(k == 1), stop=(k == K - 1))
 
                 result = results.tile([P, PIECE], F32, name="result")
                 for s in range(STEPS):

@@ -10,8 +10,9 @@ K, R = 4, 2048
 N = K * R
 L, B = 16, 128
 BLOCKS = C // P
-PIECE = 512
+PIECE = 1024
 PIECES = R // PIECE
+BANK = 512
 STEPS = PIECE // B
 
 FLOPS = 2 * C * N
@@ -50,7 +51,6 @@ def tile_progwalktokembedwithval_kernel(tc, tab, w, pe, offs, out):
         for i in range(PIECES):
             for b in range(BLOCKS):
                 total = sums.tile([P, PIECE], F32, name="total")
-                addends = []
                 for k in range(K):
                     first = (k * R + i * PIECE) // 16
                     product = products.tile([P, PIECE], F32, name="product")
@@ -60,13 +60,14 @@ def tile_progwalktokembedwithval_kernel(tc, tab, w, pe, offs, out):
                         weights[k][i][:],
                         mybir.AluOpType.mult,
                     )
-                    addends.append(product)
-                    if k == 1:
-                        pair = products.tile([P, PIECE], F32, name="pair")
-                        nc.vector.tensor_tensor(pair[:], addends[0][:], addends[1][:], mybir.AluOpType.add)
-                        addends = [pair]
-                    if k >= 1:
-                        nc.tensor.matmul(total[:], identity[:], addends[-1][:], start=(k == 1), stop=(k == K - 1))
+                    for bank in range(0, PIECE, BANK):
+                        nc.tensor.matmul(
+                            total[:, bank : bank + BANK],
+                            identity[:],
+                            product[:, bank : bank + BANK],
+                            start=(k == 0),
+                            stop=(k == K - 1),
+                        )
 
                 result = results.tile([P, PIECE], F32, name="result")
                 for s in range(STEPS):

@@ -13,7 +13,8 @@ BLOCKS = C // P
 PIECE = 1024
 PIECES = R // PIECE
 BANK = 512
-STEPS = PIECE // B
+BANKS = PIECE // BANK
+STEPS = BANK // B
 
 FLOPS = 2 * C * N
 
@@ -50,7 +51,7 @@ def tile_progwalktokembedwithval_kernel(tc, tab, w, pe, offs, out):
 
         for i in range(PIECES):
             for b in range(BLOCKS):
-                total = sums.tile([P, PIECE], F32, name="total")
+                totals = [sums.tile([P, BANK], F32, name=f"total{j}") for j in range(BANKS)]
                 for k in range(K):
                     first = (k * R + i * PIECE) // 16
                     product = products.tile([P, PIECE], F32, name="product")
@@ -60,22 +61,24 @@ def tile_progwalktokembedwithval_kernel(tc, tab, w, pe, offs, out):
                         weights[k][i][:],
                         mybir.AluOpType.mult,
                     )
-                    for bank in range(0, PIECE, BANK):
+                    for j in range(BANKS):
                         nc.tensor.matmul(
-                            total[:, bank : bank + BANK],
+                            totals[j][:],
                             identity[:],
-                            product[:, bank : bank + BANK],
+                            product[:, j * BANK : (j + 1) * BANK],
                             start=(k == 0),
                             stop=(k == K - 1),
                         )
 
-                result = results.tile([P, PIECE], F32, name="result")
-                for s in range(STEPS):
-                    step = i * STEPS + s
-                    nc.scalar.activation(
-                        result[:, s * B : (s + 1) * B],
-                        total[:, s * B : (s + 1) * B],
-                        mybir.ActivationFunctionType.Identity,
-                        bias=encodings[b][:, step : step + 1],
-                    )
-                nc.sync.dma_start(out[b * P : (b + 1) * P, i * PIECE : (i + 1) * PIECE], result[:])
+                for j in range(BANKS):
+                    position = i * PIECE + j * BANK
+                    result = results.tile([P, BANK], F32, name="result")
+                    for s in range(STEPS):
+                        step = position // B + s
+                        nc.scalar.activation(
+                            result[:, s * B : (s + 1) * B],
+                            totals[j][:, s * B : (s + 1) * B],
+                            mybir.ActivationFunctionType.Identity,
+                            bias=encodings[b][:, step : step + 1],
+                        )
+                    nc.sync.dma_start(out[b * P : (b + 1) * P, position : position + BANK], result[:])

@@ -15,6 +15,7 @@ PIECES = R // PIECE
 BANK = 512
 BANKS = PIECE // BANK
 STEPS = BANK // B
+BY_TENSOR = K - 2
 
 FLOPS = 2 * C * N
 
@@ -49,36 +50,75 @@ def tile_progwalktokembedwithval_kernel(tc, tab, w, pe, offs, out):
         identity = held.tile([P, P], F32, name="identity")
         masks.make_identity(nc, identity[:])
 
-        for i in range(PIECES):
-            for b in range(BLOCKS):
-                totals = [sums.tile([P, BANK], F32, name=f"total{j}") for j in range(BANKS)]
-                for k in range(K):
-                    first = (k * R + i * PIECE) // 16
-                    product = products.tile([P, PIECE], F32, name="product")
-                    nc.vector.tensor_tensor(
-                        product[:],
-                        tables[b][:].indirect(offsets[:, first : first + PIECE // 16]),
-                        weights[k][i][:],
-                        mybir.AluOpType.mult,
-                    )
-                    for j in range(BANKS):
-                        nc.tensor.matmul(
-                            totals[j][:],
-                            identity[:],
-                            product[:, j * BANK : (j + 1) * BANK],
-                            start=(k == 0),
-                            stop=(k == K - 1),
-                        )
+        def look_up(b, k, i, column, width):
+            first = (k * R + i * PIECE + column) // 16
+            product = products.tile([P, PIECE], F32, name="product")
+            nc.vector.tensor_tensor(
+                product[:, 0:width],
+                tables[b][:].indirect(offsets[:, first : first + width // 16]),
+                weights[k][i][:, column : column + width],
+                mybir.AluOpType.mult,
+            )
+            return product
 
+        def encode(b, position, total):
+            result = results.tile([P, BANK], F32, name="result")
+            for s in range(STEPS):
+                step = position // B + s
+                nc.scalar.activation(
+                    result[:, s * B : (s + 1) * B],
+                    total[:, s * B : (s + 1) * B],
+                    mybir.ActivationFunctionType.Identity,
+                    bias=encodings[b][:, step : step + 1],
+                )
+            return result
+
+        def store(b, position, result):
+            nc.sync.dma_start(out[b * P : (b + 1) * P, position : position + BANK], result[:])
+
+        groups = [(i, b) for i in range(PIECES) for b in range(BLOCKS)]
+        for i, b in groups[:-1]:
+            totals = [sums.tile([P, BANK], F32, name=f"total{j}") for j in range(BANKS)]
+            for k in range(K):
+                product = look_up(b, k, i, 0, PIECE)
                 for j in range(BANKS):
-                    position = i * PIECE + j * BANK
-                    result = results.tile([P, BANK], F32, name="result")
-                    for s in range(STEPS):
-                        step = position // B + s
-                        nc.scalar.activation(
-                            result[:, s * B : (s + 1) * B],
-                            totals[j][:, s * B : (s + 1) * B],
-                            mybir.ActivationFunctionType.Identity,
-                            bias=encodings[b][:, step : step + 1],
-                        )
-                    nc.sync.dma_start(out[b * P : (b + 1) * P, position : position + BANK], result[:])
+                    nc.tensor.matmul(
+                        totals[j][:],
+                        identity[:],
+                        product[:, j * BANK : (j + 1) * BANK],
+                        start=(k == 0),
+                        stop=(k == K - 1),
+                    )
+            for j in range(BANKS):
+                position = i * PIECE + j * BANK
+                store(b, position, encode(b, position, totals[j]))
+
+        i, b = groups[-1]
+        ending = BANKS - 1
+        position = i * PIECE + ending * BANK
+        totals = [sums.tile([P, BANK], F32, name=f"total{j}") for j in range(BANKS)]
+        for k in range(K - 1):
+            product = look_up(b, k, i, 0, PIECE)
+            for j in range(BANKS):
+                if j < ending or k < BY_TENSOR:
+                    nc.tensor.matmul(
+                        totals[j][:],
+                        identity[:],
+                        product[:, j * BANK : (j + 1) * BANK],
+                        start=(k == 0),
+                        stop=(j == ending and k == BY_TENSOR - 1),
+                    )
+            if k == BY_TENSOR - 1:
+                partial = encode(b, position, totals[ending])
+        third = product[:, ending * BANK : (ending + 1) * BANK]
+        for j in range(BANKS):
+            if j == ending:
+                three = results.tile([P, BANK], F32, name="three")
+                nc.vector.tensor_tensor(three[:], third, partial[:], mybir.AluOpType.add)
+            fourth = look_up(b, K - 1, i, j * BANK, BANK)
+            if j < ending:
+                nc.tensor.matmul(totals[j][:], identity[:], fourth[:, 0:BANK], start=False, stop=True)
+                store(b, i * PIECE + j * BANK, encode(b, i * PIECE + j * BANK, totals[j]))
+        whole = results.tile([P, BANK], F32, name="whole")
+        nc.vector.tensor_tensor(whole[:], three[:], fourth[:, 0:BANK], mybir.AluOpType.add)
+        store(b, position, whole)

@@ -118,7 +118,12 @@ def tile_progwalktokembedwithval_kernel(tc, tab, w, pe, offs, out):
             fourth = look_up(b, K - 1, i, j * BANK, BANK)
             if j < ending:
                 nc.tensor.matmul(totals[j][:], identity[:], fourth[:, 0:BANK], start=False, stop=True)
-                store(b, i * PIECE + j * BANK, encode(b, i * PIECE + j * BANK, totals[j]))
+                result = encode(b, i * PIECE + j * BANK, totals[j])
+                for lo in (0, BANK // 2):
+                    first = i * PIECE + j * BANK + lo
+                    nc.sync.dma_start(out[b * P : (b + 1) * P, first : first + BANK // 2], result[:, lo : lo + BANK // 2])
         whole = results.tile([P, BANK], F32, name="whole")
-        nc.vector.tensor_tensor(whole[:], three[:], fourth[:, 0:BANK], mybir.AluOpType.add)
-        store(b, position, whole)
+        for lo in (0, BANK // 2):
+            hi = lo + BANK // 2
+            nc.vector.tensor_tensor(whole[:, lo:hi], three[:, lo:hi], fourth[:, lo:hi], mybir.AluOpType.add)
+            nc.sync.dma_start(out[b * P : (b + 1) * P, position + lo : position + hi], whole[:, lo:hi])

@@ -12,6 +12,8 @@ L, B = 16, 128
 BLOCKS = C // P
 PIECE = 1024
 PIECES = R // PIECE
+ROW = 256
+ROWS = N // ROW
 BANK = 512
 BANKS = PIECE // BANK
 STEPS = BANK // B
@@ -29,7 +31,11 @@ def tile_progwalktokembedwithval_kernel(tc, tab, w, pe, offs, out):
         tc.tile_pool(name="products", bufs=4) as products,
         tc.tile_pool(name="results", bufs=2) as results,
         tc.psum_pool(name="sums", bufs=2) as sums,
+        tc.psum_pool(name="spread", bufs=2) as spread,
     ):
+        w_rows = held.tile([ROWS, ROW], F32, name="w_rows")
+        nc.scalar.dma_start(w_rows[:], w.rearrange("o (r c) -> (o r) c", c=ROW))
+
         offsets = held.tile([P, N // 16], U16, name="offsets")
         nc.sync.dma_start(offsets[:], offs)
 
@@ -41,7 +47,8 @@ def tile_progwalktokembedwithval_kernel(tc, tab, w, pe, offs, out):
         for i in range(PIECES):
             for k in range(K):
                 first = k * R + i * PIECE
-                nc.sync.dma_start(weights[k][i][:], w_row[first : first + PIECE].partition_broadcast(P))
+                done = BANK if first == 0 else 0
+                nc.sync.dma_start(weights[k][i][:, done:PIECE], w_row[first + done : first + PIECE].partition_broadcast(P))
             if i == 0:
                 nc.sync.dma_start(tables[1][:], tab[P : 2 * P, :])
                 for b in range(BLOCKS):
@@ -49,6 +56,11 @@ def tile_progwalktokembedwithval_kernel(tc, tab, w, pe, offs, out):
 
         identity = held.tile([P, P], F32, name="identity")
         masks.make_identity(nc, identity[:])
+
+        for r in range(BANK // ROW):
+            repeated = spread.tile([P, ROW], F32, name="repeated")
+            nc.tensor.matmul(repeated[:], identity[0:ROWS, r : r + 1].to_broadcast([ROWS, P]), w_rows[:])
+            nc.scalar.copy(weights[0][0][:, r * ROW : (r + 1) * ROW], repeated[:])
 
         def look_up(b, k, i, column, width):
             first = (k * R + i * PIECE + column) // 16
@@ -80,15 +92,19 @@ def tile_progwalktokembedwithval_kernel(tc, tab, w, pe, offs, out):
         for i, b in groups[:-1]:
             totals = [sums.tile([P, BANK], F32, name=f"total{j}") for j in range(BANKS)]
             for k in range(K):
-                product = look_up(b, k, i, 0, PIECE)
-                for j in range(BANKS):
-                    nc.tensor.matmul(
-                        totals[j][:],
-                        identity[:],
-                        product[:, j * BANK : (j + 1) * BANK],
-                        start=(k == 0),
-                        stop=(k == K - 1),
-                    )
+                cuts = (0, ROW, BANK, PIECE) if (i, b, k) == (0, 0, 0) else (0, PIECE)
+                for lo, hi in zip(cuts[:-1], cuts[1:]):
+                    product = look_up(b, k, i, lo, hi - lo)
+                    for column in range(lo, hi, BANK):
+                        width = min(BANK, hi - column)
+                        inside = column % BANK
+                        nc.tensor.matmul(
+                            totals[column // BANK][:, inside : inside + width],
+                            identity[:],
+                            product[:, column - lo : column - lo + width],
+                            start=(k == 0 and inside == 0),
+                            stop=(k == K - 1),
+                        )
             for j in range(BANKS):
                 position = i * PIECE + j * BANK
                 store(b, position, encode(b, position, totals[j]))

@@ -34,7 +34,7 @@ def tile_progwalktokembedwithval_kernel(tc, tab, w, pe, offs, out):
         tc.psum_pool(name="spread", bufs=2) as spread,
     ):
         w_rows = held.tile([ROWS, ROW], F32, name="w_rows")
-        nc.scalar.dma_start(w_rows[:], w.rearrange("o (r c) -> (o r) c", c=ROW))
+        nc.sync.dma_start(w_rows[:], w.rearrange("o (r c) -> (o r) c", c=ROW))
 
         offsets = held.tile([P, N // 16], U16, name="offsets")
         nc.sync.dma_start(offsets[:], offs)

@@ -16,8 +16,7 @@ ROW = 256
 ROWS = N // ROW
 BANK = 512
 BANKS = PIECE // BANK
-STEPS = BANK // B
-BY_TENSOR = K - 2
+HALF = BANK // 2
 
 FLOPS = 2 * C * N
 
@@ -28,10 +27,10 @@ def tile_progwalktokembedwithval_kernel(tc, tab, w, pe, offs, out):
 
     with (
         tc.tile_pool(name="held", bufs=1) as held,
-        tc.tile_pool(name="products", bufs=4) as products,
-        tc.tile_pool(name="results", bufs=2) as results,
+        tc.tile_pool(name="products", bufs=6) as products,
+        tc.tile_pool(name="results", bufs=4) as results,
         tc.psum_pool(name="sums", bufs=2) as sums,
-        tc.psum_pool(name="spread", bufs=2) as spread,
+        tc.psum_pool(name="in_halves", bufs=4) as in_halves,
     ):
         w_rows = held.tile([ROWS, ROW], F32, name="w_rows")
         nc.sync.dma_start(w_rows[:], w.rearrange("o (r c) -> (o r) c", c=ROW))
@@ -58,7 +57,7 @@ def tile_progwalktokembedwithval_kernel(tc, tab, w, pe, offs, out):
         masks.make_identity(nc, identity[:])
 
         for r in range(BANK // ROW):
-            repeated = spread.tile([P, ROW], F32, name="repeated")
+            repeated = in_halves.tile([P, ROW], F32, name="half")
             nc.tensor.matmul(repeated[:], identity[0:ROWS, r : r + 1].to_broadcast([ROWS, P]), w_rows[:])
             nc.scalar.copy(weights[0][0][:, r * ROW : (r + 1) * ROW], repeated[:])
 
@@ -73,9 +72,9 @@ def tile_progwalktokembedwithval_kernel(tc, tab, w, pe, offs, out):
             )
             return product
 
-        def encode(b, position, total):
+        def encode(b, position, total, width):
             result = results.tile([P, BANK], F32, name="result")
-            for s in range(STEPS):
+            for s in range(width // B):
                 step = position // B + s
                 nc.scalar.activation(
                     result[:, s * B : (s + 1) * B],
@@ -85,8 +84,8 @@ def tile_progwalktokembedwithval_kernel(tc, tab, w, pe, offs, out):
                 )
             return result
 
-        def store(b, position, result):
-            nc.sync.dma_start(out[b * P : (b + 1) * P, position : position + BANK], result[:])
+        def store(b, position, result, column, width):
+            nc.sync.dma_start(out[b * P : (b + 1) * P, position : position + width], result[:, column : column + width])
 
         groups = [(i, b) for i in range(PIECES) for b in range(BLOCKS)]
         for i, b in groups[:-1]:
@@ -107,39 +106,27 @@ def tile_progwalktokembedwithval_kernel(tc, tab, w, pe, offs, out):
                         )
             for j in range(BANKS):
                 position = i * PIECE + j * BANK
-                store(b, position, encode(b, position, totals[j]))
+                store(b, position, encode(b, position, totals[j], BANK), 0, BANK)
 
         i, b = groups[-1]
-        ending = BANKS - 1
-        position = i * PIECE + ending * BANK
-        totals = [sums.tile([P, BANK], F32, name=f"total{j}") for j in range(BANKS)]
+        first = i * PIECE
+        quarters = [in_halves.tile([P, HALF], F32, name="half") for q in range(PIECE // HALF)]
         for k in range(K - 1):
             product = look_up(b, k, i, 0, PIECE)
-            for j in range(BANKS):
-                if j < ending or k < BY_TENSOR:
-                    nc.tensor.matmul(
-                        totals[j][:],
-                        identity[:],
-                        product[:, j * BANK : (j + 1) * BANK],
-                        start=(k == 0),
-                        stop=(j == ending and k == BY_TENSOR - 1),
-                    )
-            if k == BY_TENSOR - 1:
-                partial = encode(b, position, totals[ending])
-        third = product[:, ending * BANK : (ending + 1) * BANK]
-        for j in range(BANKS):
-            if j == ending:
-                three = results.tile([P, BANK], F32, name="three")
-                nc.vector.tensor_tensor(three[:], third, partial[:], mybir.AluOpType.add)
-            fourth = look_up(b, K - 1, i, j * BANK, BANK)
-            if j < ending:
-                nc.tensor.matmul(totals[j][:], identity[:], fourth[:, 0:BANK], start=False, stop=True)
-                result = encode(b, i * PIECE + j * BANK, totals[j])
-                for lo in (0, BANK // 2):
-                    first = i * PIECE + j * BANK + lo
-                    nc.sync.dma_start(out[b * P : (b + 1) * P, first : first + BANK // 2], result[:, lo : lo + BANK // 2])
-        whole = results.tile([P, BANK], F32, name="whole")
-        for lo in (0, BANK // 2):
-            hi = lo + BANK // 2
-            nc.vector.tensor_tensor(whole[:, lo:hi], three[:, lo:hi], fourth[:, lo:hi], mybir.AluOpType.add)
-            nc.sync.dma_start(out[b * P : (b + 1) * P, position + lo : position + hi], whole[:, lo:hi])
+            for q, quarter in enumerate(quarters):
+                nc.tensor.matmul(
+                    quarter[:],
+                    identity[:],
+                    product[:, q * HALF : (q + 1) * HALF],
+                    start=(k == 0),
+                    stop=(k == K - 2),
+                )
+        sums_of_three = [encode(b, first + q * HALF, quarter, HALF) for q, quarter in enumerate(quarters)]
+        run3 = [look_up(b, K - 1, i, j * BANK, BANK) for j in range(BANKS)]
+        for q, three in enumerate(sums_of_three):
+            j, inside = divmod(q * HALF, BANK)
+            whole = results.tile([P, HALF], F32, name="whole")
+            nc.vector.tensor_tensor(
+                whole[:], three[:, 0:HALF], run3[j][:, inside : inside + HALF], mybir.AluOpType.add
+            )
+            store(b, first + q * HALF, whole, 0, HALF)

@@ -112,15 +112,17 @@ def tile_progwalktokembedwithval_kernel(tc, tab, w, pe, offs, out):
         first = i * PIECE
         quarters = [in_halves.tile([P, HALF], F32, name="half") for q in range(PIECE // HALF)]
         for k in range(K - 1):
-            product = look_up(b, k, i, 0, PIECE)
-            for q, quarter in enumerate(quarters):
-                nc.tensor.matmul(
-                    quarter[:],
-                    identity[:],
-                    product[:, q * HALF : (q + 1) * HALF],
-                    start=(k == 0),
-                    stop=(k == K - 2),
-                )
+            width = PIECE if k == 0 else BANK
+            for lo in range(0, PIECE, width):
+                product = look_up(b, k, i, lo, width)
+                for column in range(0, width, HALF):
+                    nc.tensor.matmul(
+                        quarters[(lo + column) // HALF][:],
+                        identity[:],
+                        product[:, column : column + HALF],
+                        start=(k == 0),
+                        stop=(k == K - 2),
+                    )
         sums_of_three = [encode(b, first + q * HALF, quarter, HALF) for q, quarter in enumerate(quarters)]
         run3 = [look_up(b, K - 1, i, j * BANK, BANK) for j in range(BANKS)]
         for q, three in enumerate(sums_of_three):

@@ -44,7 +44,7 @@ def tile_progwalktokembedwithval_kernel(tc, tab, w, pe, offs, out):
 
         nc.sync.dma_start(tables[0][:], tab[0:P, :])
         for i in range(PIECES):
-            for k in range(K):
+            for k in (1, 0, 2, 3) if i == 0 else range(K):
                 first = k * R + i * PIECE
                 done = BANK if first == 0 else 0
                 nc.sync.dma_start(weights[k][i][:, done:PIECE], w_row[first + done : first + PIECE].partition_broadcast(P))
@@ -90,20 +90,23 @@ def tile_progwalktokembedwithval_kernel(tc, tab, w, pe, offs, out):
         groups = [(i, b) for i in range(PIECES) for b in range(BLOCKS)]
         for i, b in groups[:-1]:
             totals = [sums.tile([P, BANK], F32, name=f"total{j}") for j in range(BANKS)]
-            for k in range(K):
-                cuts = (0, ROW, BANK, PIECE) if (i, b, k) == (0, 0, 0) else (0, PIECE)
-                for lo, hi in zip(cuts[:-1], cuts[1:]):
-                    product = look_up(b, k, i, lo, hi - lo)
-                    for column in range(lo, hi, BANK):
-                        width = min(BANK, hi - column)
-                        inside = column % BANK
-                        nc.tensor.matmul(
-                            totals[column // BANK][:, inside : inside + width],
-                            identity[:],
-                            product[:, column - lo : column - lo + width],
-                            start=(k == 0 and inside == 0),
-                            stop=(k == K - 1),
-                        )
+            look_ups = [(k, 0, PIECE) for k in range(K)]
+            if (i, b) == (0, 0):
+                look_ups[0:2] = [(0, 0, ROW), (0, ROW, BANK), (1, 0, PIECE), (0, BANK, PIECE)]
+            opened = set()
+            for k, lo, hi in look_ups:
+                product = look_up(b, k, i, lo, hi - lo)
+                for column in range(lo, hi, BANK):
+                    j, inside = divmod(column, BANK)
+                    width = min(BANK, hi - column)
+                    nc.tensor.matmul(
+                        totals[j][:, inside : inside + width],
+                        identity[:],
+                        product[:, column - lo : column - lo + width],
+                        start=(j not in opened),
+                        stop=(k == K - 1),
+                    )
+                    opened.add(j)
             for j in range(BANKS):
                 position = i * PIECE + j * BANK
                 store(b, position, encode(b, position, totals[j], BANK), 0, BANK)

import concourse.masks as masks
import concourse.mybir as mybir

F32 = mybir.dt.float32
U16 = mybir.dt.uint16

P = 128
C, S = 256, 2048
K, R = 4, 2048
N = K * R
L, B = 16, 128
BLOCKS = C // P
PIECE = 1024
PIECES = R // PIECE
ROW = 256
ROWS = N // ROW
BANK = 512
BANKS = PIECE // BANK
HALF = BANK // 2

FLOPS = 2 * C * N


def tile_progwalktokembedwithval_kernel(tc, tab, w, pe, offs, out):
    nc = tc.nc
    w_row = w.rearrange("o n -> (o n)")

    with (
        tc.tile_pool(name="held", bufs=1) as held,
        tc.tile_pool(name="products", bufs=6) as products,
        tc.tile_pool(name="results", bufs=4) as results,
        tc.psum_pool(name="sums", bufs=2) as sums,
        tc.psum_pool(name="in_halves", bufs=4) as in_halves,
    ):
        w_rows = held.tile([ROWS, ROW], F32, name="w_rows")
        nc.sync.dma_start(w_rows[:], w.rearrange("o (r c) -> (o r) c", c=ROW))

        offsets = held.tile([P, N // 16], U16, name="offsets")
        nc.sync.dma_start(offsets[:], offs)

        tables = [held.tile([P, S], F32, name=f"table{b}") for b in range(BLOCKS)]
        encodings = [held.tile([P, L], F32, name=f"encoding{b}") for b in range(BLOCKS)]
        weights = [[held.tile([P, PIECE], F32, name=f"weights{k}_{i}") for i in range(PIECES)] for k in range(K)]

        nc.sync.dma_start(tables[0][:], tab[0:P, :])
        for i in range(PIECES):
            for k in (1, 0, 2, 3) if i == 0 else range(K):
                first = k * R + i * PIECE
                done = BANK if first == 0 else 0
                nc.sync.dma_start(weights[k][i][:, done:PIECE], w_row[first + done : first + PIECE].partition_broadcast(P))
            if i == 0:
                nc.sync.dma_start(tables[1][:], tab[P : 2 * P, :])
                for b in range(BLOCKS):
                    nc.sync.dma_start(encodings[b][:], pe[b * P : (b + 1) * P, :])

        identity = held.tile([P, P], F32, name="identity")
        masks.make_identity(nc, identity[:])

        for r in range(BANK // ROW):
            repeated = in_halves.tile([P, ROW], F32, name="half")
            nc.tensor.matmul(repeated[:], identity[0:ROWS, r : r + 1].to_broadcast([ROWS, P]), w_rows[:])
            nc.scalar.copy(weights[0][0][:, r * ROW : (r + 1) * ROW], repeated[:])

        def look_up(b, k, i, column, width):
            first = (k * R + i * PIECE + column) // 16
            product = products.tile([P, PIECE], F32, name="product")
            nc.vector.tensor_tensor(
                product[:, 0:width],
                tables[b][:].indirect(offsets[:, first : first + width // 16]),
                weights[k][i][:, column : column + width],
                mybir.AluOpType.mult,
            )
            return product

        def encode(b, position, total, width):
            result = results.tile([P, BANK], F32, name="result")
            for s in range(width // B):
                step = position // B + s
                nc.scalar.activation(
                    result[:, s * B : (s + 1) * B],
                    total[:, s * B : (s + 1) * B],
                    mybir.ActivationFunctionType.Identity,
                    bias=encodings[b][:, step : step + 1],
                )
            return result

        def store(b, position, result, column, width):
            nc.sync.dma_start(out[b * P : (b + 1) * P, position : position + width], result[:, column : column + width])

        groups = [(i, b) for i in range(PIECES) for b in range(BLOCKS)]
        for i, b in groups[:-1]:
            totals = [sums.tile([P, BANK], F32, name=f"total{j}") for j in range(BANKS)]
            look_ups = [(k, 0, PIECE) for k in range(K)]
            if (i, b) == (0, 0):
                look_ups[0:2] = [(0, 0, ROW), (0, ROW, BANK), (1, 0, PIECE), (0, BANK, PIECE)]
            opened = set()
            for k, lo, hi in look_ups:
                product = look_up(b, k, i, lo, hi - lo)
                for column in range(lo, hi, BANK):
                    j, inside = divmod(column, BANK)
                    width = min(BANK, hi - column)
                    nc.tensor.matmul(
                        totals[j][:, inside : inside + width],
                        identity[:],
                        product[:, column - lo : column - lo + width],
                        start=(j not in opened),
                        stop=(k == K - 1),
                    )
                    opened.add(j)
            for j in range(BANKS):
                position = i * PIECE + j * BANK
                store(b, position, encode(b, position, totals[j], BANK), 0, BANK)

        i, b = groups[-1]
        first = i * PIECE
        quarters = [in_halves.tile([P, HALF], F32, name="half") for q in range(PIECE // HALF)]
        for k in range(K - 1):
            width = PIECE if k == 0 else BANK
            for lo in range(0, PIECE, width):
                product = look_up(b, k, i, lo, width)
                for column in range(0, width, HALF):
                    nc.tensor.matmul(
                        quarters[(lo + column) // HALF][:],
                        identity[:],
                        product[:, column : column + HALF],
                        start=(k == 0),
                        stop=(k == K - 2),
                    )
        sums_of_three = [encode(b, first + q * HALF, quarter, HALF) for q, quarter in enumerate(quarters)]
        run3 = [look_up(b, K - 1, i, j * BANK, BANK) for j in range(BANKS)]
        for q, three in enumerate(sums_of_three):
            j, inside = divmod(q * HALF, BANK)
            whole = results.tile([P, HALF], F32, name="whole")
            nc.vector.tensor_tensor(
                whole[:], three[:, 0:HALF], run3[j][:, inside : inside + HALF], mybir.AluOpType.add
            )
            store(b, first + q * HALF, whole, 0, HALF)
